import numpy as np
import ml_dtypes


def mxq(x, axis, fmt="e4m3"):
    dtype, down = {"e4m3": (ml_dtypes.float8_e4m3fn, 7), "e5m2": (ml_dtypes.float8_e5m2, 14)}[fmt]
    v = np.moveaxis(np.asarray(x, np.float32).astype(ml_dtypes.bfloat16).astype(np.float64), axis, -1)
    blocks = v.reshape(v.shape[:-1] + (-1, 32))
    amax = np.abs(blocks).max(-1, keepdims=True)
    byte = np.maximum(np.where(amax > 0, np.frexp(amax)[1] - 1 + 127, 0) - down, 1)
    scale = np.exp2(byte - 127.0)
    codes = (blocks / scale).astype(np.float32).astype(dtype).astype(np.float64)
    return np.moveaxis((codes * scale).reshape(v.shape), -1, axis)


WIDE = False


def mx_kscale(k):
    if not WIDE:
        return np.ones(k)
    levels = np.array([10, -10, 5, -5, 0])
    a = np.random.permutation(np.resize(levels, k // 512 * 4)).reshape(k // 512, 4)
    idx = np.arange(k)
    return np.exp2(a[idx // 512, idx % 128 // 32])


BF16 = ml_dtypes.bfloat16


def bf(x):
    return np.asarray(x, np.float32).astype(BF16)


def f64(x):
    return np.asarray(x).astype(np.float64)


B, L, F, D, N = 4096, 32, 512, 512, 512
EPS = 1e-12


def setup_inputs():
    s = mx_kscale(D)
    v = np.random.standard_normal((B, D)) * 2.0
    pooled = np.where(v > 0.0, v, np.exp(np.minimum(v, 0.0)) - 1.0)
    return {"pooled": bf(pooled * s),
            "lin_w": bf(np.random.standard_normal((D, D)) / np.sqrt(D) / s),
            "lin_b": bf(np.random.standard_normal(D) * 0.2),
            "embed_weight": bf(np.random.standard_normal((N, D)) * 2.0)}


def reference(pooled, lin_w, lin_b, embed_weight):
    out2 = np.maximum((mxq(f64(pooled), 1, "e4m3") @ mxq(f64(lin_w), 1, "e4m3").T) + f64(lin_b), 0.0)
    xn = out2 / np.maximum(np.sqrt((out2 ** 2).sum(axis=1, keepdims=True)), EPS)
    table = f64(embed_weight)[:N]
    logits = mxq(xn, 1, "e4m3") @ mxq(table, 1, "e4m3").T
    e = np.exp(logits - logits.max(axis=1, keepdims=True))
    return e / e.sum(axis=1, keepdims=True)

@@ -1,0 +1,256 @@
+from contextlib import ExitStack
+
+import concourse.mybir as mybir
+from concourse.masks import make_identity
+
+F32 = mybir.dt.float32
+BF16 = mybir.dt.bfloat16
+U32 = mybir.dt.uint32
+U8 = mybir.dt.uint8
+FP8X4 = mybir.dt.float8_e4m3fn_x4
+ACT = mybir.ActivationFunctionType
+ALU = mybir.AluOpType
+
+P = 128
+PACK = 4
+DEPTH = P * PACK
+ROWS = 4096
+BLOCK = 512
+TILES = BLOCK // P
+BLOCKS = ROWS // BLOCK
+UNITS = ROWS // P
+BANKS = 8
+EPS = 1e-12
+
+FLOPS = 2 * 2 * ROWS * DEPTH * DEPTH
+
+LAG_REGROUP = 1
+LAG_QUANT = 2
+LAG_HIDDEN = 6
+LAG_EMBED = 5
+LAG_BACK = 10
+LAG_NORM = 11
+LAG_SPREAD = 12
+LAG_XN = 13
+LAG_LOGITS = 14
+LAG_SOFTMAX = 15
+LAG_STORE = 16
+STEPS = UNITS + LAG_STORE
+
+
+def due(step, lag, count):
+    return 0 <= step - lag < count
+
+
+def tile_conceptembedmodel_pb_t_kernel(tc, pooled, lin_w, lin_b, embed_weight, out):
+    nc = tc.nc
+    pooled_blocks = pooled.rearrange("(b p c) k -> b p c k", p=P, c=TILES)
+    out_blocks = out.rearrange("(b p c) n -> b p c n", p=P, c=TILES)
+
+    with ExitStack() as ctx:
+        ctx.enter_context(tc.manual_schedule())
+        const = ctx.enter_context(tc.tile_pool(name="const", bufs=1))
+        inputs = ctx.enter_context(tc.tile_pool(name="inputs", bufs=BLOCKS))
+        stage = ctx.enter_context(tc.tile_pool(name="stage", bufs=4))
+        operands = ctx.enter_context(tc.tile_pool(name="operands", bufs=3))
+        hidden = ctx.enter_context(tc.tile_pool(name="hidden", bufs=3))
+        small = ctx.enter_context(tc.tile_pool(name="small", bufs=4))
+        results = ctx.enter_context(tc.tile_pool(name="results", bufs=6))
+        psum = ctx.enter_context(tc.psum_pool(name="psum", bufs=BANKS))
+
+        ident = const.tile([P, P], F32)
+        make_identity(nc, ident[:])
+        minus_half = const.tile([P, 1], F32)
+        nc.gpsimd.memset(minus_half[:], -0.5)
+
+        bias_bf16 = const.tile([P, TILES], BF16)
+        nc.scalar.dma_start(
+            out=bias_bf16[:].rearrange("p (u e) -> p u e", u=2),
+            in_=lin_b.rearrange("(u p e) -> p u e", u=2, p=P, e=2),
+        )
+        bias = const.tile([P, TILES], F32)
+        nc.vector.tensor_copy(out=bias[:], in_=bias_bf16[:])
+        warm = const.tile([P, 1], F32)
+        nc.scalar.activation(out=warm[:], in_=minus_half[:], func=ACT.Exp)
+
+        w_rows = const.tile([P, TILES, DEPTH], BF16)
+        nc.sync.dma_start(
+            out=w_rows[:].rearrange("p (u e) k -> p u e k", u=2),
+            in_=lin_w.rearrange("(u p e) k -> p u e k", u=2, p=P, e=2),
+        )
+        x_rows = []
+        for b in range(BLOCKS):
+            x_rows.append(inputs.tile([P, TILES, DEPTH], BF16, name="x_rows"))
+        for b in range(2):
+            nc.sync.dma_start(out=x_rows[b][:], in_=pooled_blocks[b])
+        e_rows = const.tile([P, TILES, DEPTH], BF16)
+        nc.sync.dma_start(out=e_rows[:], in_=embed_weight.rearrange("(c p) d -> p c d", p=P))
+        for b in range(2, BLOCKS):
+            nc.sync.dma_start(out=x_rows[b][:], in_=pooled_blocks[b])
+
+        w_codes = const.tile([P, BLOCK], U32, align_bytes=64)
+        w_scales = const.tile([P, BLOCK], U8, align_bytes=64)
+        e_codes = const.tile([P, BLOCK], U32, align_bytes=64)
+        e_scales = const.tile([P, BLOCK], U8, align_bytes=64)
+
+        w_flipped, e_flipped, x_flipped = {}, {}, {}
+        w_grouped, e_grouped, x_grouped = {}, {}, {}
+        x_codes, x_scales = {}, {}
+        h, h_rows, inv_norm, spread = {}, {}, {}, {}
+        xn, xn_codes, xn_scales = {}, {}, {}
+        logits, neg_max, probs, exp_sum = {}, {}, {}, {}
+
+        def flip(rows, c):
+            words = rows.rearrange("p c k -> p (c k)").bitcast(F32).rearrange("p (c w) -> p c w", c=TILES)
+            flipped = psum.tile([P, 2, P], F32, name="flipped", tag="bank")
+            for u in range(2):
+                nc.tensor.transpose(flipped[:, u, :], words[:, c, u * P : (u + 1) * P], ident[:])
+            return flipped
+
+        def regroup(flipped, on_scalar):
+            grouped = stage.tile([P, P * PACK], BF16, name="grouped", bufs=8, align_bytes=64)
+            grouped_words = grouped[:].bitcast(F32).rearrange("q (n u) -> q n u", u=2)
+            if on_scalar:
+                nc.scalar.copy(out=grouped_words, in_=flipped[:].rearrange("q u n -> q n u"))
+            else:
+                nc.vector.tensor_copy(out=grouped_words, in_=flipped[:].rearrange("q u n -> q n u"))
+            return grouped
+
+        def quantise(grouped, codes, scales, c):
+            nc.vector.quantize_mx(
+                out=codes[:, c * P : (c + 1) * P].bitcast(FP8X4),
+                scales=scales[:, c * P : (c + 1) * P],
+                in_=grouped[:],
+            )
+
+        def quantise_pooled(t):
+            b, c = divmod(t, TILES)
+            if c == 0:
+                x_codes[b] = operands.tile([P, BLOCK], U32, name="x_codes", align_bytes=64)
+                x_scales[b] = operands.tile([P, BLOCK], U8, name="x_scales", align_bytes=64)
+            quantise(x_grouped[t], x_codes[b], x_scales[b], c)
+
+        def first_matmul_and_relu(b, j):
+            if j == 0:
+                h[b] = hidden.tile([P, TILES, BLOCK], F32, name="h")
+            sums = psum.tile([P, BLOCK], F32, name="sums", tag="bank")
+            nc.tensor.matmul_mx(
+                out=sums[:],
+                lhsT=w_codes[:, j * P : (j + 1) * P].bitcast(FP8X4),
+                lhsT_scale=w_scales[:, j * P : (j + 1) * P],
+                rhs=x_codes[b][:].bitcast(FP8X4),
+                rhs_scale=x_scales[b][:],
+                start=True,
+                stop=True,
+            )
+            nc.scalar.activation(out=h[b][:, j, :], in_=sums[:], func=ACT.Relu, bias=bias[:, j : j + 1], scale=1.0)
+
+        def transpose_back(t):
+            b, c = divmod(t, TILES)
+            h_rows[t] = psum.tile([P, TILES, P], F32, name="h_rows", tag="bank")
+            for j in range(TILES):
+                nc.tensor.transpose(h_rows[t][:, j, :], h[b][:, j, c * P : (c + 1) * P], ident[:])
+
+        def reciprocal_norm(t):
+            squares = stage.tile([P, BLOCK], BF16, name="squares")
+            sum_sq = small.tile([P, 1], F32, name="sum_sq")
+            nc.scalar.activation(
+                out=squares[:], in_=h_rows[t][:].rearrange("p j d -> p (j d)"), func=ACT.Square, accum_out=sum_sq[:]
+            )
+            floored = small.tile([P, 1], F32, name="floored")
+            nc.gpsimd.tensor_scalar_max(out=floored[:], in0=sum_sq[:], scalar1=EPS * EPS)
+            inv_norm[t] = small.tile([P, 1], F32, name="inv_norm")
+            nc.gpsimd.tensor_tensor(out=inv_norm[t][:], in0=floored[:], in1=minus_half[:], op=ALU.pow)
+
+        def spread_norm(t):
+            spread[t] = psum.tile([P, P], F32, name="spread", tag="bank")
+            nc.tensor.matmul(
+                out=spread[t][:], lhsT=inv_norm[t][:].to_broadcast([P, P]), rhs=ident[:], start=True, stop=True
+            )
+
+        def scale_hidden(t):
+            b, c = divmod(t, TILES)
+            xn[t] = stage.tile([P, P * PACK], BF16, name="xn", align_bytes=64)
+            nc.vector.tensor_tensor(
+                out=xn[t][:].rearrange("p (n j) -> p n j", j=PACK),
+                in0=h[b][:, :, c * P : (c + 1) * P].rearrange("p j n -> p n j"),
+                in1=spread[t][:].unsqueeze(2).to_broadcast([P, P, PACK]),
+                op=ALU.mult,
+            )
+
+        def quantise_xn(t):
+            xn_codes[t] = operands.tile([P, P], U32, name="xn_codes", align_bytes=64)
+            xn_scales[t] = operands.tile([P, P], U8, name="xn_scales", align_bytes=64)
+            quantise(xn[t], xn_codes[t], xn_scales[t], 0)
+
+        def second_matmul(t):
+            logits[t] = psum.tile([P, BLOCK], F32, name="logits", tag="bank")
+            nc.tensor.matmul_mx(
+                out=logits[t][:],
+                lhsT=xn_codes[t][:].bitcast(FP8X4),
+                lhsT_scale=xn_scales[t][:],
+                rhs=e_codes[:].bitcast(FP8X4),
+                rhs_scale=e_scales[:],
+                start=True,
+                stop=True,
+            )
+
+        def row_maximum(t):
+            neg_max[t] = small.tile([P, 1], F32, name="neg_max")
+            nc.vector.tensor_reduce(
+                out=neg_max[t][:], in_=logits[t][:], axis=mybir.AxisListType.X, op=ALU.max, negate=True
+            )
+
+        def exponentials(t):
+            probs[t] = results.tile([P, BLOCK], F32, name="probs")
+            exp_sum[t] = small.tile([P, 1], F32, name="exp_sum")
+            nc.scalar.activation(
+                out=probs[t][:], in_=logits[t][:], func=ACT.Exp, bias=neg_max[t][:], scale=1.0, accum_out=exp_sum[t][:]
+            )
+
+        def divide_and_store(t):
+            b, c = divmod(t, TILES)
+            inv_sum = small.tile([P, 1], F32, name="inv_sum")
+            nc.vector.reciprocal(out=inv_sum[:], in_=exp_sum[t][:])
+            nc.vector.tensor_scalar_mul(out=probs[t][:], in0=probs[t][:], scalar1=inv_sum[:])
+            nc.sync.dma_start(out=out_blocks[b][:, c, :], in_=probs[t][:])
+
+        for step in range(STEPS):
+            if due(step, LAG_SOFTMAX, UNITS):
+                row_maximum(step - LAG_SOFTMAX)
+            if due(step, LAG_STORE, UNITS):
+                divide_and_store(step - LAG_STORE)
+            if due(step, LAG_NORM, UNITS):
+                reciprocal_norm(step - LAG_NORM)
+            if due(step, LAG_HIDDEN, UNITS):
+                first_matmul_and_relu((step - LAG_HIDDEN) // TILES, (step - LAG_HIDDEN) % TILES)
+            if due(step, LAG_LOGITS, UNITS):
+                second_matmul(step - LAG_LOGITS)
+            if due(step, LAG_SPREAD, UNITS):
+                spread_norm(step - LAG_SPREAD)
+            if due(step, LAG_XN, UNITS):
+                scale_hidden(step - LAG_XN)
+            if due(step, LAG_SOFTMAX, UNITS):
+                exponentials(step - LAG_SOFTMAX)
+            if due(step, LAG_BACK, UNITS):
+                transpose_back(step - LAG_BACK)
+            if due(step, LAG_QUANT, TILES):
+                quantise(w_grouped[step - LAG_QUANT], w_codes, w_scales, step - LAG_QUANT)
+            if due(step, LAG_QUANT, UNITS):
+                quantise_pooled(step - LAG_QUANT)
+            if due(step, LAG_EMBED + LAG_QUANT, TILES):
+                quantise(e_grouped[step - LAG_EMBED - LAG_QUANT], e_codes, e_scales, step - LAG_EMBED - LAG_QUANT)
+            if due(step, 0, TILES):
+                w_flipped[step] = flip(w_rows[:], step)
+            if due(step, 0, UNITS):
+                x_flipped[step] = flip(x_rows[step // TILES][:], step % TILES)
+            if due(step, LAG_EMBED, TILES):
+                e_flipped[step - LAG_EMBED] = flip(e_rows[:], step - LAG_EMBED)
+            if due(step, LAG_REGROUP, TILES):
+                w_grouped[step - LAG_REGROUP] = regroup(w_flipped[step - LAG_REGROUP], step % 2 == 0)
+            if due(step, LAG_REGROUP, UNITS):
+                x_grouped[step - LAG_REGROUP] = regroup(x_flipped[step - LAG_REGROUP], step % 2 == 1)
+            if due(step, LAG_EMBED + LAG_REGROUP, TILES):
+                e_grouped[step - LAG_EMBED - LAG_REGROUP] = regroup(e_flipped[step - LAG_EMBED - LAG_REGROUP], False)
+            if due(step, LAG_XN, UNITS):
+                quantise_xn(step - LAG_XN)

@@ -19,6 +19,8 @@ BLOCK = 512
 TILES = BLOCK // P
 BLOCKS = ROWS // BLOCK
 UNITS = ROWS // P
+PAIR = 2 * P
+PAIRS = ROWS // PAIR
 BANKS = 8
 EPS = 1e-12
 
@@ -26,16 +28,17 @@ FLOPS = 2 * 2 * ROWS * DEPTH * DEPTH
 
 LAG_REGROUP = 1
 LAG_QUANT = 2
-LAG_HIDDEN = 6
-LAG_EMBED = 5
-LAG_BACK = 10
-LAG_NORM = 11
-LAG_SPREAD = 12
-LAG_XN = 13
-LAG_LOGITS = 14
-LAG_SOFTMAX = 15
-LAG_STORE = 16
+LAG_HIDDEN = 4
+LAG_EMBED = 4
+LAG_BACK = 8
+LAG_NORM = 9
+LAG_SPREAD = 10
+LAG_XN = 11
+LAG_LOGITS = 12
+LAG_SOFTMAX = 13
+LAG_STORE = 14
 STEPS = UNITS + LAG_STORE
+VECTOR_PAIRS = 8
 
 
 def due(step, lag, count):
@@ -92,43 +95,39 @@ def tile_conceptembedmodel_pb_t_kernel(tc, pooled, lin_w, lin_b, embed_weight, o
         w_scales = const.tile([P, BLOCK], U8, align_bytes=64)
         e_codes = const.tile([P, BLOCK], U32, align_bytes=64)
         e_scales = const.tile([P, BLOCK], U8, align_bytes=64)
+        x_codes, x_scales = [], []
+        for b in range(BLOCKS):
+            x_codes.append(inputs.tile([P, BLOCK], U32, name="x_codes", align_bytes=64))
+            x_scales.append(inputs.tile([P, BLOCK], U8, name="x_scales", align_bytes=64))
 
         w_flipped, e_flipped, x_flipped = {}, {}, {}
         w_grouped, e_grouped, x_grouped = {}, {}, {}
-        x_codes, x_scales = {}, {}
         h, h_rows, inv_norm, spread = {}, {}, {}, {}
         xn, xn_codes, xn_scales = {}, {}, {}
-        logits, neg_max, probs, exp_sum = {}, {}, {}, {}
+        logits, neg_max, probs, exp_sum, inv_sum = {}, {}, {}, {}, {}
 
-        def flip(rows, c):
+        def flip(rows, half):
             words = rows.rearrange("p c k -> p (c k)").bitcast(F32).rearrange("p (c w) -> p c w", c=TILES)
-            flipped = psum.tile([P, 2, P], F32, name="flipped", tag="bank")
+            flipped = psum.tile([P, 2, PAIR], F32, name="flipped", tag="bank")
             for u in range(2):
-                nc.tensor.transpose(flipped[:, u, :], words[:, c, u * P : (u + 1) * P], ident[:])
+                for c in range(2):
+                    nc.tensor.transpose(
+                        flipped[:, u, c * P : (c + 1) * P], words[:, 2 * half + c, u * P : (u + 1) * P], ident[:]
+                    )
             return flipped
 
-        def regroup(flipped, on_scalar):
-            grouped = stage.tile([P, P * PACK], BF16, name="grouped", bufs=8, align_bytes=64)
-            grouped_words = grouped[:].bitcast(F32).rearrange("q (n u) -> q n u", u=2)
+        def regroup(flipped, grouped, half, on_scalar):
+            columns = grouped[:].bitcast(F32).rearrange("q (n u) -> q n u", u=2)[:, half * PAIR : (half + 1) * PAIR, :]
             if on_scalar:
-                nc.scalar.copy(out=grouped_words, in_=flipped[:].rearrange("q u n -> q n u"))
+                nc.scalar.copy(out=columns, in_=flipped[:].rearrange("q u n -> q n u"))
             else:
-                nc.vector.tensor_copy(out=grouped_words, in_=flipped[:].rearrange("q u n -> q n u"))
-            return grouped
+                nc.vector.tensor_copy(out=columns, in_=flipped[:].rearrange("q u n -> q n u"))
 
-        def quantise(grouped, codes, scales, c):
-            nc.vector.quantize_mx(
-                out=codes[:, c * P : (c + 1) * P].bitcast(FP8X4),
-                scales=scales[:, c * P : (c + 1) * P],
-                in_=grouped[:],
-            )
+        def new_grouped():
+            return stage.tile([P, BLOCK * PACK], BF16, name="grouped", align_bytes=64)
 
-        def quantise_pooled(t):
-            b, c = divmod(t, TILES)
-            if c == 0:
-                x_codes[b] = operands.tile([P, BLOCK], U32, name="x_codes", align_bytes=64)
-                x_scales[b] = operands.tile([P, BLOCK], U8, name="x_scales", align_bytes=64)
-            quantise(x_grouped[t], x_codes[b], x_scales[b], c)
+        def quantise(values, codes, scales):
+            nc.vector.quantize_mx(out=codes[:].bitcast(FP8X4), scales=scales[:], in_=values[:])
 
         def first_matmul_and_relu(b, j):
             if j == 0:
@@ -181,7 +180,7 @@ def tile_conceptembedmodel_pb_t_kernel(tc, pooled, lin_w, lin_b, embed_weight, o
         def quantise_xn(t):
             xn_codes[t] = operands.tile([P, P], U32, name="xn_codes", align_bytes=64)
             xn_scales[t] = operands.tile([P, P], U8, name="xn_scales", align_bytes=64)
-            quantise(xn[t], xn_codes[t], xn_scales[t], 0)
+            quantise(xn[t], xn_codes[t], xn_scales[t])
 
         def second_matmul(t):
             logits[t] = psum.tile([P, BLOCK], F32, name="logits", tag="bank")
@@ -208,18 +207,20 @@ def tile_conceptembedmodel_pb_t_kernel(tc, pooled, lin_w, lin_b, embed_weight, o
                 out=probs[t][:], in_=logits[t][:], func=ACT.Exp, bias=neg_max[t][:], scale=1.0, accum_out=exp_sum[t][:]
             )
 
+        def reciprocal_sum(t):
+            inv_sum[t] = small.tile([P, 1], F32, name="inv_sum")
+            nc.vector.reciprocal(out=inv_sum[t][:], in_=exp_sum[t][:])
+
         def divide_and_store(t):
             b, c = divmod(t, TILES)
-            inv_sum = small.tile([P, 1], F32, name="inv_sum")
-            nc.vector.reciprocal(out=inv_sum[:], in_=exp_sum[t][:])
-            nc.vector.tensor_scalar_mul(out=probs[t][:], in0=probs[t][:], scalar1=inv_sum[:])
+            nc.vector.tensor_scalar_mul(out=probs[t][:], in0=probs[t][:], scalar1=inv_sum[t][:])
             nc.sync.dma_start(out=out_blocks[b][:, c, :], in_=probs[t][:])
 
         for step in range(STEPS):
+            if due(step, LAG_STORE, UNITS):
+                reciprocal_sum(step - LAG_STORE)
             if due(step, LAG_SOFTMAX, UNITS):
                 row_maximum(step - LAG_SOFTMAX)
-            if due(step, LAG_STORE, UNITS):
-                divide_and_store(step - LAG_STORE)
             if due(step, LAG_NORM, UNITS):
                 reciprocal_norm(step - LAG_NORM)
             if due(step, LAG_HIDDEN, UNITS):
@@ -230,27 +231,37 @@ def tile_conceptembedmodel_pb_t_kernel(tc, pooled, lin_w, lin_b, embed_weight, o
                 spread_norm(step - LAG_SPREAD)
             if due(step, LAG_XN, UNITS):
                 scale_hidden(step - LAG_XN)
+            if due(step, LAG_STORE, UNITS):
+                divide_and_store(step - LAG_STORE)
             if due(step, LAG_SOFTMAX, UNITS):
                 exponentials(step - LAG_SOFTMAX)
             if due(step, LAG_BACK, UNITS):
                 transpose_back(step - LAG_BACK)
-            if due(step, LAG_QUANT, TILES):
-                quantise(w_grouped[step - LAG_QUANT], w_codes, w_scales, step - LAG_QUANT)
-            if due(step, LAG_QUANT, UNITS):
-                quantise_pooled(step - LAG_QUANT)
-            if due(step, LAG_EMBED + LAG_QUANT, TILES):
-                quantise(e_grouped[step - LAG_EMBED - LAG_QUANT], e_codes, e_scales, step - LAG_EMBED - LAG_QUANT)
-            if due(step, 0, TILES):
+
+            if step == LAG_QUANT + 1:
+                quantise(w_grouped[0], w_codes, w_scales)
+            if due(step, LAG_QUANT, PAIRS) and (step - LAG_QUANT) % 2 == 1:
+                quantise(x_grouped[(step - LAG_QUANT) // 2], x_codes[(step - LAG_QUANT) // 2], x_scales[(step - LAG_QUANT) // 2])
+            if step == LAG_EMBED + LAG_QUANT + 1:
+                quantise(e_grouped[0], e_codes, e_scales)
+            if due(step, 0, 2):
                 w_flipped[step] = flip(w_rows[:], step)
-            if due(step, 0, UNITS):
-                x_flipped[step] = flip(x_rows[step // TILES][:], step % TILES)
-            if due(step, LAG_EMBED, TILES):
+            if due(step, 0, PAIRS):
+                x_flipped[step] = flip(x_rows[step // 2][:], step % 2)
+            if due(step, LAG_EMBED, 2):
                 e_flipped[step - LAG_EMBED] = flip(e_rows[:], step - LAG_EMBED)
-            if due(step, LAG_REGROUP, TILES):
-                w_grouped[step - LAG_REGROUP] = regroup(w_flipped[step - LAG_REGROUP], step % 2 == 0)
-            if due(step, LAG_REGROUP, UNITS):
-                x_grouped[step - LAG_REGROUP] = regroup(x_flipped[step - LAG_REGROUP], step % 2 == 1)
-            if due(step, LAG_EMBED + LAG_REGROUP, TILES):
-                e_grouped[step - LAG_EMBED - LAG_REGROUP] = regroup(e_flipped[step - LAG_EMBED - LAG_REGROUP], False)
+            if due(step, LAG_REGROUP, 2):
+                if step == LAG_REGROUP:
+                    w_grouped[0] = new_grouped()
+                regroup(w_flipped[step - LAG_REGROUP], w_grouped[0], step - LAG_REGROUP, True)
+            if due(step, LAG_REGROUP, PAIRS):
+                pair = step - LAG_REGROUP
+                if pair % 2 == 0:
+                    x_grouped[pair // 2] = new_grouped()
+                regroup(x_flipped[pair], x_grouped[pair // 2], pair % 2, pair >= VECTOR_PAIRS)
+            if due(step, LAG_EMBED + LAG_REGROUP, 2):
+                if step == LAG_EMBED + LAG_REGROUP:
+                    e_grouped[0] = new_grouped()
+                regroup(e_flipped[step - LAG_EMBED - LAG_REGROUP], e_grouped[0], step - LAG_EMBED - LAG_REGROUP, False)
             if due(step, LAG_XN, UNITS):
                 quantise_xn(step - LAG_XN)

@@ -32,13 +32,12 @@ LAG_HIDDEN = 4
 LAG_EMBED = 4
 LAG_BACK = 8
 LAG_NORM = 9
-LAG_SPREAD = 10
-LAG_XN = 11
-LAG_LOGITS = 12
-LAG_SOFTMAX = 13
-LAG_STORE = 14
+LAG_SPREAD = 11
+LAG_XN = 12
+LAG_LOGITS = 13
+LAG_SOFTMAX = 14
+LAG_STORE = 15
 STEPS = UNITS + LAG_STORE
-VECTOR_PAIRS = 8
 
 
 def due(step, lag, count):
@@ -213,14 +212,20 @@ def tile_conceptembedmodel_pb_t_kernel(tc, pooled, lin_w, lin_b, embed_weight, o
 
         def divide_and_store(t):
             b, c = divmod(t, TILES)
-            nc.vector.tensor_scalar_mul(out=probs[t][:], in0=probs[t][:], scalar1=inv_sum[t][:])
+            nc.gpsimd.tensor_scalar(
+                out=probs[t][:], in0=probs[t][:], scalar1=inv_sum[t][:], scalar2=0.0, op0=ALU.mult, op1=ALU.add
+            )
             nc.sync.dma_start(out=out_blocks[b][:, c, :], in_=probs[t][:])
 
+        for half in range(2):
+            w_flipped[half] = flip(w_rows[:], half)
+
         for step in range(STEPS):
-            if due(step, LAG_STORE, UNITS):
-                reciprocal_sum(step - LAG_STORE)
             if due(step, LAG_SOFTMAX, UNITS):
                 row_maximum(step - LAG_SOFTMAX)
+            if due(step, LAG_STORE, UNITS):
+                reciprocal_sum(step - LAG_STORE)
+                divide_and_store(step - LAG_STORE)
             if due(step, LAG_NORM, UNITS):
                 reciprocal_norm(step - LAG_NORM)
             if due(step, LAG_HIDDEN, UNITS):
@@ -231,8 +236,6 @@ def tile_conceptembedmodel_pb_t_kernel(tc, pooled, lin_w, lin_b, embed_weight, o
                 spread_norm(step - LAG_SPREAD)
             if due(step, LAG_XN, UNITS):
                 scale_hidden(step - LAG_XN)
-            if due(step, LAG_STORE, UNITS):
-                divide_and_store(step - LAG_STORE)
             if due(step, LAG_SOFTMAX, UNITS):
                 exponentials(step - LAG_SOFTMAX)
             if due(step, LAG_BACK, UNITS):
@@ -244,8 +247,6 @@ def tile_conceptembedmodel_pb_t_kernel(tc, pooled, lin_w, lin_b, embed_weight, o
                 quantise(x_grouped[(step - LAG_QUANT) // 2], x_codes[(step - LAG_QUANT) // 2], x_scales[(step - LAG_QUANT) // 2])
             if step == LAG_EMBED + LAG_QUANT + 1:
                 quantise(e_grouped[0], e_codes, e_scales)
-            if due(step, 0, 2):
-                w_flipped[step] = flip(w_rows[:], step)
             if due(step, 0, PAIRS):
                 x_flipped[step] = flip(x_rows[step // 2][:], step % 2)
             if due(step, LAG_EMBED, 2):
@@ -258,7 +259,7 @@ def tile_conceptembedmodel_pb_t_kernel(tc, pooled, lin_w, lin_b, embed_weight, o
                 pair = step - LAG_REGROUP
                 if pair % 2 == 0:
                     x_grouped[pair // 2] = new_grouped()
-                regroup(x_flipped[pair], x_grouped[pair // 2], pair % 2, pair >= VECTOR_PAIRS)
+                regroup(x_flipped[pair], x_grouped[pair // 2], pair % 2, pair % 2 == 1)
             if due(step, LAG_EMBED + LAG_REGROUP, 2):
                 if step == LAG_EMBED + LAG_REGROUP:
                     e_grouped[0] = new_grouped()

@@ -23,6 +23,7 @@ PAIR = 2 * P
 PAIRS = ROWS // PAIR
 BANKS = 8
 EPS = 1e-12
+RUN = 4
 
 FLOPS = 2 * 2 * ROWS * DEPTH * DEPTH
 
@@ -32,12 +33,13 @@ LAG_HIDDEN = 4
 LAG_EMBED = 4
 LAG_BACK = 8
 LAG_NORM = 9
-LAG_SPREAD = 11
-LAG_XN = 12
-LAG_LOGITS = 13
-LAG_SOFTMAX = 14
-LAG_STORE = 15
+LAG_SPREAD = 10
+LAG_XN = 11
+LAG_LOGITS = 12
+LAG_SOFTMAX = 13
+LAG_STORE = 14
 STEPS = UNITS + LAG_STORE
+VECTOR_PAIRS = 8
 
 
 def due(step, lag, count):
@@ -170,9 +172,9 @@ def tile_conceptembedmodel_pb_t_kernel(tc, pooled, lin_w, lin_b, embed_weight, o
             b, c = divmod(t, TILES)
             xn[t] = stage.tile([P, P * PACK], BF16, name="xn", align_bytes=64)
             nc.vector.tensor_tensor(
-                out=xn[t][:].rearrange("p (n j) -> p n j", j=PACK),
-                in0=h[b][:, :, c * P : (c + 1) * P].rearrange("p j n -> p n j"),
-                in1=spread[t][:].unsqueeze(2).to_broadcast([P, P, PACK]),
+                out=xn[t][:].rearrange("p (g i j) -> p g j i", i=RUN, j=PACK),
+                in0=h[b][:, :, c * P : (c + 1) * P].rearrange("p j (g i) -> p g j i", i=RUN),
+                in1=spread[t][:].rearrange("p (g i) -> p g i", i=RUN).unsqueeze(2).to_broadcast([P, P // RUN, PACK, RUN]),
                 op=ALU.mult,
             )
 
@@ -212,20 +214,14 @@ def tile_conceptembedmodel_pb_t_kernel(tc, pooled, lin_w, lin_b, embed_weight, o
 
         def divide_and_store(t):
             b, c = divmod(t, TILES)
-            nc.gpsimd.tensor_scalar(
-                out=probs[t][:], in0=probs[t][:], scalar1=inv_sum[t][:], scalar2=0.0, op0=ALU.mult, op1=ALU.add
-            )
+            nc.vector.tensor_scalar_mul(out=probs[t][:], in0=probs[t][:], scalar1=inv_sum[t][:])
             nc.sync.dma_start(out=out_blocks[b][:, c, :], in_=probs[t][:])
 
-        for half in range(2):
-            w_flipped[half] = flip(w_rows[:], half)
-
         for step in range(STEPS):
-            if due(step, LAG_SOFTMAX, UNITS):
-                row_maximum(step - LAG_SOFTMAX)
             if due(step, LAG_STORE, UNITS):
                 reciprocal_sum(step - LAG_STORE)
-                divide_and_store(step - LAG_STORE)
+            if due(step, LAG_SOFTMAX, UNITS):
+                row_maximum(step - LAG_SOFTMAX)
             if due(step, LAG_NORM, UNITS):
                 reciprocal_norm(step - LAG_NORM)
             if due(step, LAG_HIDDEN, UNITS):
@@ -236,6 +232,8 @@ def tile_conceptembedmodel_pb_t_kernel(tc, pooled, lin_w, lin_b, embed_weight, o
                 spread_norm(step - LAG_SPREAD)
             if due(step, LAG_XN, UNITS):
                 scale_hidden(step - LAG_XN)
+            if due(step, LAG_STORE, UNITS):
+                divide_and_store(step - LAG_STORE)
             if due(step, LAG_SOFTMAX, UNITS):
                 exponentials(step - LAG_SOFTMAX)
             if due(step, LAG_BACK, UNITS):
@@ -247,6 +245,8 @@ def tile_conceptembedmodel_pb_t_kernel(tc, pooled, lin_w, lin_b, embed_weight, o
                 quantise(x_grouped[(step - LAG_QUANT) // 2], x_codes[(step - LAG_QUANT) // 2], x_scales[(step - LAG_QUANT) // 2])
             if step == LAG_EMBED + LAG_QUANT + 1:
                 quantise(e_grouped[0], e_codes, e_scales)
+            if due(step, 0, 2):
+                w_flipped[step] = flip(w_rows[:], step)
             if due(step, 0, PAIRS):
                 x_flipped[step] = flip(x_rows[step // 2][:], step % 2)
             if due(step, LAG_EMBED, 2):
@@ -259,7 +259,7 @@ def tile_conceptembedmodel_pb_t_kernel(tc, pooled, lin_w, lin_b, embed_weight, o
                 pair = step - LAG_REGROUP
                 if pair % 2 == 0:
                     x_grouped[pair // 2] = new_grouped()
-                regroup(x_flipped[pair], x_grouped[pair // 2], pair % 2, pair % 2 == 1)
+                regroup(x_flipped[pair], x_grouped[pair // 2], pair % 2, pair >= VECTOR_PAIRS)
             if due(step, LAG_EMBED + LAG_REGROUP, 2):
                 if step == LAG_EMBED + LAG_REGROUP:
                     e_grouped[0] = new_grouped()

@@ -27,19 +27,9 @@ RUN = 4
 
 FLOPS = 2 * 2 * ROWS * DEPTH * DEPTH
 
-LAG_REGROUP = 1
-LAG_QUANT = 2
-LAG_HIDDEN = 4
-LAG_EMBED = 4
-LAG_BACK = 8
-LAG_NORM = 9
-LAG_SPREAD = 10
-LAG_XN = 11
-LAG_LOGITS = 12
-LAG_SOFTMAX = 13
-LAG_STORE = 14
-STEPS = UNITS + LAG_STORE
-VECTOR_PAIRS = 8
+HIDDEN_AHEAD = 6
+STEPS = UNITS + 7
+PSUM_BUFS = {"flipped": 1, "sums": 2, "h_rows": 1, "spread": 1, "logits": 3}
 
 
 def due(step, lag, count):
@@ -55,11 +45,11 @@ def tile_conceptembedmodel_pb_t_kernel(tc, pooled, lin_w, lin_b, embed_weight, o
         ctx.enter_context(tc.manual_schedule())
         const = ctx.enter_context(tc.tile_pool(name="const", bufs=1))
         inputs = ctx.enter_context(tc.tile_pool(name="inputs", bufs=BLOCKS))
-        stage = ctx.enter_context(tc.tile_pool(name="stage", bufs=4))
+        stage = ctx.enter_context(tc.tile_pool(name="stage", bufs=6))
         operands = ctx.enter_context(tc.tile_pool(name="operands", bufs=3))
-        hidden = ctx.enter_context(tc.tile_pool(name="hidden", bufs=3))
-        small = ctx.enter_context(tc.tile_pool(name="small", bufs=4))
-        results = ctx.enter_context(tc.tile_pool(name="results", bufs=6))
+        hidden = ctx.enter_context(tc.tile_pool(name="hidden", bufs=4))
+        small = ctx.enter_context(tc.tile_pool(name="small", bufs=8))
+        results = ctx.enter_context(tc.tile_pool(name="results", bufs=8))
         psum = ctx.enter_context(tc.psum_pool(name="psum", bufs=BANKS))
 
         ident = const.tile([P, P], F32)
@@ -78,18 +68,21 @@ def tile_conceptembedmodel_pb_t_kernel(tc, pooled, lin_w, lin_b, embed_weight, o
         nc.scalar.activation(out=warm[:], in_=minus_half[:], func=ACT.Exp)
 
         w_rows = const.tile([P, TILES, DEPTH], BF16)
-        nc.sync.dma_start(
-            out=w_rows[:].rearrange("p (u e) k -> p u e k", u=2),
-            in_=lin_w.rearrange("(u p e) k -> p u e k", u=2, p=P, e=2),
-        )
         x_rows = []
         for b in range(BLOCKS):
             x_rows.append(inputs.tile([P, TILES, DEPTH], BF16, name="x_rows"))
-        for b in range(2):
+        for u in range(2):
+            nc.sync.dma_start(
+                out=w_rows[:, 2 * u : 2 * u + 2, :], in_=lin_w.rearrange("(u p e) k -> u p e k", u=2, p=P, e=2)[u]
+            )
+            nc.sync.dma_start(
+                out=x_rows[0][:, 2 * u : 2 * u + 2, :], in_=pooled_blocks[0][:, 2 * u : 2 * u + 2, :]
+            )
+        for b in range(1, 3):
             nc.sync.dma_start(out=x_rows[b][:], in_=pooled_blocks[b])
         e_rows = const.tile([P, TILES, DEPTH], BF16)
         nc.sync.dma_start(out=e_rows[:], in_=embed_weight.rearrange("(c p) d -> p c d", p=P))
-        for b in range(2, BLOCKS):
+        for b in range(3, BLOCKS):
             nc.sync.dma_start(out=x_rows[b][:], in_=pooled_blocks[b])
 
         w_codes = const.tile([P, BLOCK], U32, align_bytes=64)
@@ -103,13 +96,14 @@ def tile_conceptembedmodel_pb_t_kernel(tc, pooled, lin_w, lin_b, embed_weight, o
 
         w_flipped, e_flipped, x_flipped = {}, {}, {}
         w_grouped, e_grouped, x_grouped = {}, {}, {}
-        h, h_rows, inv_norm, spread = {}, {}, {}, {}
+        sums, h, h_rows, inv_norm, spread = {}, {}, {}, {}, {}
         xn, xn_codes, xn_scales = {}, {}, {}
         logits, neg_max, probs, exp_sum, inv_sum = {}, {}, {}, {}, {}
+        sums2 = {}
 
-        def flip(rows, half):
+        def flip(rows, half, tag="flipped"):
             words = rows.rearrange("p c k -> p (c k)").bitcast(F32).rearrange("p (c w) -> p c w", c=TILES)
-            flipped = psum.tile([P, 2, PAIR], F32, name="flipped", tag="bank")
+            flipped = psum.tile([P, 2, PAIR], F32, name="flipped", tag=tag, bufs=PSUM_BUFS[tag])
             for u in range(2):
                 for c in range(2):
                     nc.tensor.transpose(
@@ -130,12 +124,40 @@ def tile_conceptembedmodel_pb_t_kernel(tc, pooled, lin_w, lin_b, embed_weight, o
         def quantise(values, codes, scales):
             nc.vector.quantize_mx(out=codes[:].bitcast(FP8X4), scales=scales[:], in_=values[:])
 
-        def first_matmul_and_relu(b, j):
-            if j == 0:
-                h[b] = hidden.tile([P, TILES, BLOCK], F32, name="h")
-            sums = psum.tile([P, BLOCK], F32, name="sums", tag="bank")
+        def quantise_pair(pair):
+            b, half = divmod(pair, 2)
+            cols = slice(half * PAIR, (half + 1) * PAIR)
+            nc.vector.quantize_mx(
+                out=x_codes[b][:, cols].bitcast(FP8X4),
+                scales=x_scales[b][:, cols],
+                in_=x_grouped[b][:, half * PAIR * PACK : (half + 1) * PAIR * PACK],
+            )
+
+        def flip_pair(pair, tag="flipped"):
+            x_flipped[pair] = flip(x_rows[pair // 2][:], pair % 2, tag)
+
+        def regroup_tile(tile, on_scalar):
+            pair, c = divmod(tile, 2)
+            if tile % 4 == 0:
+                x_grouped[pair // 2] = new_grouped()
+            first = (tile % 4) * P
+            columns = x_grouped[pair // 2][:].bitcast(F32).rearrange("q (n u) -> q n u", u=2)[:, first : first + P, :]
+            words = x_flipped[pair][:].rearrange("q u n -> q n u")[:, c * P : (c + 1) * P, :]
+            if on_scalar:
+                nc.scalar.copy(out=columns, in_=words)
+            else:
+                nc.vector.tensor_copy(out=columns, in_=words)
+
+        def regroup_pair(pair, on_scalar=False):
+            if pair % 2 == 0:
+                x_grouped[pair // 2] = new_grouped()
+            regroup(x_flipped[pair], x_grouped[pair // 2], pair % 2, on_scalar)
+
+        def first_matmul(unit):
+            b, j = divmod(unit, TILES)
+            sums[unit] = psum.tile([P, BLOCK], F32, name="sums", tag="sums", bufs=PSUM_BUFS["sums"])
             nc.tensor.matmul_mx(
-                out=sums[:],
+                out=sums[unit][:],
                 lhsT=w_codes[:, j * P : (j + 1) * P].bitcast(FP8X4),
                 lhsT_scale=w_scales[:, j * P : (j + 1) * P],
                 rhs=x_codes[b][:].bitcast(FP8X4),
@@ -143,11 +165,16 @@ def tile_conceptembedmodel_pb_t_kernel(tc, pooled, lin_w, lin_b, embed_weight, o
                 start=True,
                 stop=True,
             )
-            nc.scalar.activation(out=h[b][:, j, :], in_=sums[:], func=ACT.Relu, bias=bias[:, j : j + 1], scale=1.0)
+
+        def relu(unit):
+            b, j = divmod(unit, TILES)
+            if j == 0:
+                h[b] = hidden.tile([P, TILES, BLOCK], F32, name="h")
+            nc.scalar.activation(out=h[b][:, j, :], in_=sums[unit][:], func=ACT.Relu, bias=bias[:, j : j + 1], scale=1.0)
 
         def transpose_back(t):
             b, c = divmod(t, TILES)
-            h_rows[t] = psum.tile([P, TILES, P], F32, name="h_rows", tag="bank")
+            h_rows[t] = psum.tile([P, TILES, P], F32, name="h_rows", tag="h_rows", bufs=PSUM_BUFS["h_rows"])
             for j in range(TILES):
                 nc.tensor.transpose(h_rows[t][:, j, :], h[b][:, j, c * P : (c + 1) * P], ident[:])
 
@@ -163,7 +190,7 @@ def tile_conceptembedmodel_pb_t_kernel(tc, pooled, lin_w, lin_b, embed_weight, o
             nc.gpsimd.tensor_tensor(out=inv_norm[t][:], in0=floored[:], in1=minus_half[:], op=ALU.pow)
 
         def spread_norm(t):
-            spread[t] = psum.tile([P, P], F32, name="spread", tag="bank")
+            spread[t] = psum.tile([P, P], F32, name="spread", tag="spread", bufs=PSUM_BUFS["spread"])
             nc.tensor.matmul(
                 out=spread[t][:], lhsT=inv_norm[t][:].to_broadcast([P, P]), rhs=ident[:], start=True, stop=True
             )
@@ -184,7 +211,7 @@ def tile_conceptembedmodel_pb_t_kernel(tc, pooled, lin_w, lin_b, embed_weight, o
             quantise(xn[t], xn_codes[t], xn_scales[t])
 
         def second_matmul(t):
-            logits[t] = psum.tile([P, BLOCK], F32, name="logits", tag="bank")
+            logits[t] = psum.tile([P, BLOCK], F32, name="logits", tag="logits", bufs=PSUM_BUFS["logits"])
             nc.tensor.matmul_mx(
                 out=logits[t][:],
                 lhsT=xn_codes[t][:].bitcast(FP8X4),
@@ -203,66 +230,99 @@ def tile_conceptembedmodel_pb_t_kernel(tc, pooled, lin_w, lin_b, embed_weight, o
 
         def exponentials(t):
             probs[t] = results.tile([P, BLOCK], F32, name="probs")
-            exp_sum[t] = small.tile([P, 1], F32, name="exp_sum")
+            if t % 2 == 0:
+                sums2[t // 2] = small.tile([P, 2], F32, name="exp_sum")
+            exp_sum[t] = sums2[t // 2][:, t % 2 : t % 2 + 1]
             nc.scalar.activation(
-                out=probs[t][:], in_=logits[t][:], func=ACT.Exp, bias=neg_max[t][:], scale=1.0, accum_out=exp_sum[t][:]
+                out=probs[t][:], in_=logits[t][:], func=ACT.Exp, bias=neg_max[t][:], scale=1.0, accum_out=exp_sum[t]
             )
 
-        def reciprocal_sum(t):
-            inv_sum[t] = small.tile([P, 1], F32, name="inv_sum")
-            nc.vector.reciprocal(out=inv_sum[t][:], in_=exp_sum[t][:])
+        def reciprocal_sums(t):
+            both = small.tile([P, 2], F32, name="inv_sum")
+            nc.vector.reciprocal(out=both[:], in_=sums2[t // 2][:])
+            for i in range(2):
+                inv_sum[t + i] = both[:, i : i + 1]
 
         def divide_and_store(t):
             b, c = divmod(t, TILES)
-            nc.vector.tensor_scalar_mul(out=probs[t][:], in0=probs[t][:], scalar1=inv_sum[t][:])
+            nc.vector.tensor_scalar_mul(out=probs[t][:], in0=probs[t][:], scalar1=inv_sum[t])
             nc.sync.dma_start(out=out_blocks[b][:, c, :], in_=probs[t][:])
 
-        for step in range(STEPS):
-            if due(step, LAG_STORE, UNITS):
-                reciprocal_sum(step - LAG_STORE)
-            if due(step, LAG_SOFTMAX, UNITS):
-                row_maximum(step - LAG_SOFTMAX)
-            if due(step, LAG_NORM, UNITS):
-                reciprocal_norm(step - LAG_NORM)
-            if due(step, LAG_HIDDEN, UNITS):
-                first_matmul_and_relu((step - LAG_HIDDEN) // TILES, (step - LAG_HIDDEN) % TILES)
-            if due(step, LAG_LOGITS, UNITS):
-                second_matmul(step - LAG_LOGITS)
-            if due(step, LAG_SPREAD, UNITS):
-                spread_norm(step - LAG_SPREAD)
-            if due(step, LAG_XN, UNITS):
-                scale_hidden(step - LAG_XN)
-            if due(step, LAG_STORE, UNITS):
-                divide_and_store(step - LAG_STORE)
-            if due(step, LAG_SOFTMAX, UNITS):
-                exponentials(step - LAG_SOFTMAX)
-            if due(step, LAG_BACK, UNITS):
-                transpose_back(step - LAG_BACK)
+        w_flipped[0] = flip(w_rows[:], 0, "logits")
+        flip_pair(0, "sums")
+        w_flipped[1] = flip(w_rows[:], 1, "logits")
+        flip_pair(1, "sums")
+        flip_pair(2, "logits")
+        flip_pair(3, "flipped")
+        w_grouped[0] = new_grouped()
+        regroup(w_flipped[0], w_grouped[0], 0, True)
+        regroup(w_flipped[1], w_grouped[0], 1, True)
+        regroup_pair(0)
+        regroup_pair(1, True)
+        quantise(w_grouped[0], w_codes, w_scales)
+        quantise_pair(0)
+        quantise_pair(1)
+        regroup_pair(2)
+        regroup_pair(3)
+        quantise_pair(2)
+        quantise_pair(3)
+        first_matmul(0)
+        relu(0)
+        first_matmul(1)
+        relu(1)
+        flip_pair(4, "logits")
+        first_matmul(2)
+        relu(2)
+        first_matmul(3)
+        relu(3)
+        flip_pair(5, "logits")
+        first_matmul(4)
+        relu(4)
+        first_matmul(5)
+        relu(5)
+        transpose_back(0)
+        e_flipped[0] = flip(e_rows[:], 0, "logits")
+        first_matmul(6)
+        e_flipped[1] = flip(e_rows[:], 1, "flipped")
+        regroup_pair(4)
+        regroup_pair(5)
+        quantise_pair(4)
+        quantise_pair(5)
+        e_grouped[0] = new_grouped()
+        regroup(e_flipped[0], e_grouped[0], 0, False)
+        regroup(e_flipped[1], e_grouped[0], 1, False)
+        flip_pair(6, "logits")
+        quantise(e_grouped[0], e_codes, e_scales)
 
-            if step == LAG_QUANT + 1:
-                quantise(w_grouped[0], w_codes, w_scales)
-            if due(step, LAG_QUANT, PAIRS) and (step - LAG_QUANT) % 2 == 1:
-                quantise(x_grouped[(step - LAG_QUANT) // 2], x_codes[(step - LAG_QUANT) // 2], x_scales[(step - LAG_QUANT) // 2])
-            if step == LAG_EMBED + LAG_QUANT + 1:
-                quantise(e_grouped[0], e_codes, e_scales)
-            if due(step, 0, 2):
-                w_flipped[step] = flip(w_rows[:], step)
-            if due(step, 0, PAIRS):
-                x_flipped[step] = flip(x_rows[step // 2][:], step % 2)
-            if due(step, LAG_EMBED, 2):
-                e_flipped[step - LAG_EMBED] = flip(e_rows[:], step - LAG_EMBED)
-            if due(step, LAG_REGROUP, 2):
-                if step == LAG_REGROUP:
-                    w_grouped[0] = new_grouped()
-                regroup(w_flipped[step - LAG_REGROUP], w_grouped[0], step - LAG_REGROUP, True)
-            if due(step, LAG_REGROUP, PAIRS):
-                pair = step - LAG_REGROUP
-                if pair % 2 == 0:
-                    x_grouped[pair // 2] = new_grouped()
-                regroup(x_flipped[pair], x_grouped[pair // 2], pair % 2, pair >= VECTOR_PAIRS)
-            if due(step, LAG_EMBED + LAG_REGROUP, 2):
-                if step == LAG_EMBED + LAG_REGROUP:
-                    e_grouped[0] = new_grouped()
-                regroup(e_flipped[step - LAG_EMBED - LAG_REGROUP], e_grouped[0], step - LAG_EMBED - LAG_REGROUP, False)
-            if due(step, LAG_XN, UNITS):
-                quantise_xn(step - LAG_XN)
+        for step in range(STEPS):
+            if due(step, 2, UNITS):
+                scale_hidden(step - 2)
+            if due(step, 0, UNITS):
+                reciprocal_norm(step)
+            if due(step, 5, UNITS):
+                exponentials(step - 5)
+            if due(step, -HIDDEN_AHEAD, UNITS):
+                relu(step + HIDDEN_AHEAD)
+            if due(step, 4, UNITS):
+                row_maximum(step - 4)
+            if due(step, 3, UNITS):
+                second_matmul(step - 3)
+            if due(step, -HIDDEN_AHEAD - 1, UNITS):
+                first_matmul(step + HIDDEN_AHEAD + 1)
+            if due(step, 1, UNITS):
+                spread_norm(step - 1)
+            if due(step, 7, UNITS):
+                divide_and_store(step - 7)
+            tile = step + 12
+            if tile < UNITS:
+                regroup_tile(tile, tile % 2 == 0)
+            if due(step, -1, UNITS):
+                transpose_back(step + 1)
+            if tile % 2 == 1 and tile + 1 < UNITS:
+                flip_pair((tile + 1) // 2)
+            if tile % 2 == 0 and tile - 2 < UNITS and tile>=14:
+                quantise_pair(tile // 2 - 1)
+            if due(step, 2, UNITS):
+                quantise_xn(step - 2)
+            if due(step, 6, UNITS) and step % 2 == 0:
+                reciprocal_sums(step - 6)

@@ -71,13 +71,15 @@ def tile_conceptembedmodel_pb_t_kernel(tc, pooled, lin_w, lin_b, embed_weight, o
         x_rows = []
         for b in range(BLOCKS):
             x_rows.append(inputs.tile([P, TILES, DEPTH], BF16, name="x_rows"))
-        for u in range(2):
+        def load_w(u):
             nc.sync.dma_start(
                 out=w_rows[:, 2 * u : 2 * u + 2, :], in_=lin_w.rearrange("(u p e) k -> u p e k", u=2, p=P, e=2)[u]
             )
-            nc.sync.dma_start(
-                out=x_rows[0][:, 2 * u : 2 * u + 2, :], in_=pooled_blocks[0][:, 2 * u : 2 * u + 2, :]
-            )
+
+        load_w(0)
+        for c in range(2):
+            nc.sync.dma_start(out=x_rows[0][:, 2 * c : 2 * c + 2, :], in_=pooled_blocks[0][:, 2 * c : 2 * c + 2, :])
+        load_w(1)
         for b in range(1, 3):
             nc.sync.dma_start(out=x_rows[b][:], in_=pooled_blocks[b])
         e_rows = const.tile([P, TILES, DEPTH], BF16)
@@ -124,14 +126,16 @@ def tile_conceptembedmodel_pb_t_kernel(tc, pooled, lin_w, lin_b, embed_weight, o
         def quantise(values, codes, scales):
             nc.vector.quantize_mx(out=codes[:].bitcast(FP8X4), scales=scales[:], in_=values[:])
 
-        def quantise_pair(pair):
-            b, half = divmod(pair, 2)
+        def quantise_half(values, codes, scales, half):
             cols = slice(half * PAIR, (half + 1) * PAIR)
             nc.vector.quantize_mx(
-                out=x_codes[b][:, cols].bitcast(FP8X4),
-                scales=x_scales[b][:, cols],
-                in_=x_grouped[b][:, half * PAIR * PACK : (half + 1) * PAIR * PACK],
+                out=codes[:, cols].bitcast(FP8X4),
+                scales=scales[:, cols],
+                in_=values[:, half * PAIR * PACK : (half + 1) * PAIR * PACK],
             )
+
+        def quantise_pair(pair):
+            quantise_half(x_grouped[pair // 2], x_codes[pair // 2], x_scales[pair // 2], pair % 2)
 
         def flip_pair(pair, tag="flipped"):
             x_flipped[pair] = flip(x_rows[pair // 2][:], pair % 2, tag)
@@ -245,37 +249,43 @@ def tile_conceptembedmodel_pb_t_kernel(tc, pooled, lin_w, lin_b, embed_weight, o
 
         def divide_and_store(t):
             b, c = divmod(t, TILES)
-            nc.vector.tensor_scalar_mul(out=probs[t][:], in0=probs[t][:], scalar1=inv_sum[t])
+            if t >= 20 and t % 2 == 0:
+                nc.scalar.activation(out=probs[t][:], in_=probs[t][:], func=ACT.Copy, scale=inv_sum[t])
+            else:
+                nc.vector.tensor_scalar_mul(out=probs[t][:], in0=probs[t][:], scalar1=inv_sum[t])
             nc.sync.dma_start(out=out_blocks[b][:, c, :], in_=probs[t][:])
 
+        w_grouped[0] = new_grouped()
+        e_grouped[0] = new_grouped()
         w_flipped[0] = flip(w_rows[:], 0, "logits")
         flip_pair(0, "sums")
-        w_flipped[1] = flip(w_rows[:], 1, "logits")
         flip_pair(1, "sums")
-        flip_pair(2, "logits")
-        flip_pair(3, "flipped")
-        w_grouped[0] = new_grouped()
+        w_flipped[1] = flip(w_rows[:], 1, "logits")
         regroup(w_flipped[0], w_grouped[0], 0, True)
-        regroup(w_flipped[1], w_grouped[0], 1, True)
-        regroup_pair(0)
+        regroup_pair(0, False)
         regroup_pair(1, True)
-        quantise(w_grouped[0], w_codes, w_scales)
+        quantise_half(w_grouped[0], w_codes, w_scales, 0)
         quantise_pair(0)
         quantise_pair(1)
-        regroup_pair(2)
-        regroup_pair(3)
-        quantise_pair(2)
-        quantise_pair(3)
+        regroup(w_flipped[1], w_grouped[0], 1, True)
+        quantise_half(w_grouped[0], w_codes, w_scales, 1)
+        flip_pair(2, "logits")
         first_matmul(0)
         relu(0)
         first_matmul(1)
         relu(1)
-        flip_pair(4, "logits")
+        flip_pair(3, "flipped")
+        regroup_pair(2, False)
+        regroup_pair(3, False)
+        quantise_pair(2)
+        quantise_pair(3)
         first_matmul(2)
         relu(2)
         first_matmul(3)
         relu(3)
+        flip_pair(4, "logits")
         flip_pair(5, "logits")
+        regroup_pair(4, False)
         first_matmul(4)
         relu(4)
         first_matmul(5)
@@ -284,11 +294,9 @@ def tile_conceptembedmodel_pb_t_kernel(tc, pooled, lin_w, lin_b, embed_weight, o
         e_flipped[0] = flip(e_rows[:], 0, "logits")
         first_matmul(6)
         e_flipped[1] = flip(e_rows[:], 1, "flipped")
-        regroup_pair(4)
-        regroup_pair(5)
+        regroup_pair(5, False)
         quantise_pair(4)
         quantise_pair(5)
-        e_grouped[0] = new_grouped()
         regroup(e_flipped[0], e_grouped[0], 0, False)
         regroup(e_flipped[1], e_grouped[0], 1, False)
         flip_pair(6, "logits")

@@ -32,6 +32,10 @@ STEPS = UNITS + 7
 PSUM_BUFS = {"flipped": 1, "sums": 2, "h_rows": 1, "spread": 1, "logits": 3}
 
 
+def on_gpsimd(t):
+    return t % 2 == 0 and t < 28
+
+
 def due(step, lag, count):
     return 0 <= step - lag < count
 
@@ -54,6 +58,15 @@ def tile_conceptembedmodel_pb_t_kernel(tc, pooled, lin_w, lin_b, embed_weight, o
 
         ident = const.tile([P, P], F32)
         make_identity(nc, ident[:])
+        zeros = const.tile([P, BLOCK], BF16)
+        nc.vector.memset(zeros[:], 0.0)
+        warm_up = psum.tile([P, BLOCK], F32, name="warm_up", tag="sums", bufs=PSUM_BUFS["sums"])
+
+        def keep_busy():
+            nc.tensor.matmul(out=warm_up[:], lhsT=zeros[:, 0:P], rhs=zeros[:], start=True, stop=True)
+
+        for i in range(5):
+            keep_busy()
         minus_half = const.tile([P, 1], F32)
         nc.gpsimd.memset(minus_half[:], -0.5)
 
@@ -157,9 +170,9 @@ def tile_conceptembedmodel_pb_t_kernel(tc, pooled, lin_w, lin_b, embed_weight, o
                 x_grouped[pair // 2] = new_grouped()
             regroup(x_flipped[pair], x_grouped[pair // 2], pair % 2, on_scalar)
 
-        def first_matmul(unit):
+        def first_matmul(unit, tag="sums"):
             b, j = divmod(unit, TILES)
-            sums[unit] = psum.tile([P, BLOCK], F32, name="sums", tag="sums", bufs=PSUM_BUFS["sums"])
+            sums[unit] = psum.tile([P, BLOCK], F32, name="sums", tag=tag, bufs=PSUM_BUFS[tag])
             nc.tensor.matmul_mx(
                 out=sums[unit][:],
                 lhsT=w_codes[:, j * P : (j + 1) * P].bitcast(FP8X4),
@@ -249,7 +262,11 @@ def tile_conceptembedmodel_pb_t_kernel(tc, pooled, lin_w, lin_b, embed_weight, o
 
         def divide_and_store(t):
             b, c = divmod(t, TILES)
-            if t >= 20 and t % 2 == 0:
+            if on_gpsimd(t):
+                nc.gpsimd.tensor_scalar(
+                    out=probs[t][:], in0=probs[t][:], scalar1=inv_sum[t], scalar2=0.0, op0=ALU.mult, op1=ALU.add
+                )
+            elif 24 <= t < 28:
                 nc.scalar.activation(out=probs[t][:], in_=probs[t][:], func=ACT.Copy, scale=inv_sum[t])
             else:
                 nc.vector.tensor_scalar_mul(out=probs[t][:], in0=probs[t][:], scalar1=inv_sum[t])
@@ -258,8 +275,11 @@ def tile_conceptembedmodel_pb_t_kernel(tc, pooled, lin_w, lin_b, embed_weight, o
         w_grouped[0] = new_grouped()
         e_grouped[0] = new_grouped()
         w_flipped[0] = flip(w_rows[:], 0, "logits")
-        flip_pair(0, "sums")
-        flip_pair(1, "sums")
+        keep_busy()
+        flip_pair(0, "flipped")
+        keep_busy()
+        flip_pair(1, "h_rows")
+        keep_busy()
         w_flipped[1] = flip(w_rows[:], 1, "logits")
         regroup(w_flipped[0], w_grouped[0], 0, True)
         regroup_pair(0, False)
@@ -270,39 +290,42 @@ def tile_conceptembedmodel_pb_t_kernel(tc, pooled, lin_w, lin_b, embed_weight, o
         regroup(w_flipped[1], w_grouped[0], 1, True)
         quantise_half(w_grouped[0], w_codes, w_scales, 1)
         flip_pair(2, "logits")
+        flip_pair(3, "flipped")
         first_matmul(0)
         relu(0)
         first_matmul(1)
         relu(1)
-        flip_pair(3, "flipped")
+        first_matmul(2, "logits")
+        relu(2)
+        first_matmul(3, "logits")
+        relu(3)
         regroup_pair(2, False)
         regroup_pair(3, False)
         quantise_pair(2)
         quantise_pair(3)
-        first_matmul(2)
-        relu(2)
-        first_matmul(3)
-        relu(3)
         flip_pair(4, "logits")
-        flip_pair(5, "logits")
-        regroup_pair(4, False)
+        flip_pair(5, "spread")
         first_matmul(4)
         relu(4)
         first_matmul(5)
         relu(5)
         transpose_back(0)
-        e_flipped[0] = flip(e_rows[:], 0, "logits")
-        first_matmul(6)
-        e_flipped[1] = flip(e_rows[:], 1, "flipped")
+        regroup_pair(4, False)
         regroup_pair(5, False)
         quantise_pair(4)
         quantise_pair(5)
+        e_flipped[0] = flip(e_rows[:], 0, "logits")
+        e_flipped[1] = flip(e_rows[:], 1, "flipped")
+        first_matmul(6)
         regroup(e_flipped[0], e_grouped[0], 0, False)
         regroup(e_flipped[1], e_grouped[0], 1, False)
         flip_pair(6, "logits")
         quantise(e_grouped[0], e_codes, e_scales)
 
         for step in range(STEPS):
+            tile = step + 12
+            if due(step, 7, UNITS) and on_gpsimd(step - 7):
+                divide_and_store(step - 7)
             if due(step, 2, UNITS):
                 scale_hidden(step - 2)
             if due(step, 0, UNITS):
@@ -319,16 +342,15 @@ def tile_conceptembedmodel_pb_t_kernel(tc, pooled, lin_w, lin_b, embed_weight, o
                 first_matmul(step + HIDDEN_AHEAD + 1)
             if due(step, 1, UNITS):
                 spread_norm(step - 1)
-            if due(step, 7, UNITS):
+            if due(step, 7, UNITS) and not on_gpsimd(step - 7):
                 divide_and_store(step - 7)
-            tile = step + 12
             if tile < UNITS:
                 regroup_tile(tile, tile % 2 == 0)
             if due(step, -1, UNITS):
                 transpose_back(step + 1)
             if tile % 2 == 1 and tile + 1 < UNITS:
                 flip_pair((tile + 1) // 2)
-            if tile % 2 == 0 and tile - 2 < UNITS and tile>=14:
+            if tile % 2 == 0 and 14 <= tile < UNITS + 2:
                 quantise_pair(tile // 2 - 1)
             if due(step, 2, UNITS):
                 quantise_xn(step - 2)

from contextlib import ExitStack

import concourse.mybir as mybir
from concourse.masks import make_identity

F32 = mybir.dt.float32
BF16 = mybir.dt.bfloat16
U32 = mybir.dt.uint32
U8 = mybir.dt.uint8
FP8X4 = mybir.dt.float8_e4m3fn_x4
ACT = mybir.ActivationFunctionType
ALU = mybir.AluOpType

P = 128
PACK = 4
DEPTH = P * PACK
ROWS = 4096
BLOCK = 512
TILES = BLOCK // P
BLOCKS = ROWS // BLOCK
UNITS = ROWS // P
PAIR = 2 * P
PAIRS = ROWS // PAIR
BANKS = 8
EPS = 1e-12
RUN = 4

FLOPS = 2 * 2 * ROWS * DEPTH * DEPTH

HIDDEN_AHEAD = 6
STEPS = UNITS + 7
PSUM_BUFS = {"flipped": 1, "sums": 2, "h_rows": 1, "spread": 1, "logits": 3}


def on_gpsimd(t):
    return t % 2 == 0 and t < 28


def due(step, lag, count):
    return 0 <= step - lag < count


def tile_conceptembedmodel_pb_t_kernel(tc, pooled, lin_w, lin_b, embed_weight, out):
    nc = tc.nc
    pooled_blocks = pooled.rearrange("(b p c) k -> b p c k", p=P, c=TILES)
    out_blocks = out.rearrange("(b p c) n -> b p c n", p=P, c=TILES)

    with ExitStack() as ctx:
        ctx.enter_context(tc.manual_schedule())
        const = ctx.enter_context(tc.tile_pool(name="const", bufs=1))
        inputs = ctx.enter_context(tc.tile_pool(name="inputs", bufs=BLOCKS))
        stage = ctx.enter_context(tc.tile_pool(name="stage", bufs=6))
        operands = ctx.enter_context(tc.tile_pool(name="operands", bufs=3))
        hidden = ctx.enter_context(tc.tile_pool(name="hidden", bufs=4))
        small = ctx.enter_context(tc.tile_pool(name="small", bufs=8))
        results = ctx.enter_context(tc.tile_pool(name="results", bufs=8))
        psum = ctx.enter_context(tc.psum_pool(name="psum", bufs=BANKS))

        ident = const.tile([P, P], F32)
        make_identity(nc, ident[:])
        zeros = const.tile([P, BLOCK], BF16)
        nc.vector.memset(zeros[:], 0.0)
        warm_up = psum.tile([P, BLOCK], F32, name="warm_up", tag="sums", bufs=PSUM_BUFS["sums"])

        def keep_busy():
            nc.tensor.matmul(out=warm_up[:], lhsT=zeros[:, 0:P], rhs=zeros[:], start=True, stop=True)

        for i in range(5):
            keep_busy()
        minus_half = const.tile([P, 1], F32)
        nc.gpsimd.memset(minus_half[:], -0.5)

        bias_bf16 = const.tile([P, TILES], BF16)
        nc.scalar.dma_start(
            out=bias_bf16[:].rearrange("p (u e) -> p u e", u=2),
            in_=lin_b.rearrange("(u p e) -> p u e", u=2, p=P, e=2),
        )
        bias = const.tile([P, TILES], F32)
        nc.vector.tensor_copy(out=bias[:], in_=bias_bf16[:])
        warm = const.tile([P, 1], F32)
        nc.scalar.activation(out=warm[:], in_=minus_half[:], func=ACT.Exp)

        w_rows = const.tile([P, TILES, DEPTH], BF16)
        x_rows = []
        for b in range(BLOCKS):
            x_rows.append(inputs.tile([P, TILES, DEPTH], BF16, name="x_rows"))
        def load_w(u):
            nc.sync.dma_start(
                out=w_rows[:, 2 * u : 2 * u + 2, :], in_=lin_w.rearrange("(u p e) k -> u p e k", u=2, p=P, e=2)[u]
            )

        load_w(0)
        for c in range(2):
            nc.sync.dma_start(out=x_rows[0][:, 2 * c : 2 * c + 2, :], in_=pooled_blocks[0][:, 2 * c : 2 * c + 2, :])
        load_w(1)
        for b in range(1, 3):
            nc.sync.dma_start(out=x_rows[b][:], in_=pooled_blocks[b])
        e_rows = const.tile([P, TILES, DEPTH], BF16)
        nc.sync.dma_start(out=e_rows[:], in_=embed_weight.rearrange("(c p) d -> p c d", p=P))
        for b in range(3, BLOCKS):
            nc.sync.dma_start(out=x_rows[b][:], in_=pooled_blocks[b])

        w_codes = const.tile([P, BLOCK], U32, align_bytes=64)
        w_scales = const.tile([P, BLOCK], U8, align_bytes=64)
        e_codes = const.tile([P, BLOCK], U32, align_bytes=64)
        e_scales = const.tile([P, BLOCK], U8, align_bytes=64)
        x_codes, x_scales = [], []
        for b in range(BLOCKS):
            x_codes.append(inputs.tile([P, BLOCK], U32, name="x_codes", align_bytes=64))
            x_scales.append(inputs.tile([P, BLOCK], U8, name="x_scales", align_bytes=64))

        w_flipped, e_flipped, x_flipped = {}, {}, {}
        w_grouped, e_grouped, x_grouped = {}, {}, {}
        sums, h, h_rows, inv_norm, spread = {}, {}, {}, {}, {}
        xn, xn_codes, xn_scales = {}, {}, {}
        logits, neg_max, probs, exp_sum, inv_sum = {}, {}, {}, {}, {}
        sums2 = {}

        def flip(rows, half, tag="flipped"):
            words = rows.rearrange("p c k -> p (c k)").bitcast(F32).rearrange("p (c w) -> p c w", c=TILES)
            flipped = psum.tile([P, 2, PAIR], F32, name="flipped", tag=tag, bufs=PSUM_BUFS[tag])
            for u in range(2):
                for c in range(2):
                    nc.tensor.transpose(
                        flipped[:, u, c * P : (c + 1) * P], words[:, 2 * half + c, u * P : (u + 1) * P], ident[:]
                    )
            return flipped

        def regroup(flipped, grouped, half, on_scalar):
            columns = grouped[:].bitcast(F32).rearrange("q (n u) -> q n u", u=2)[:, half * PAIR : (half + 1) * PAIR, :]
            if on_scalar:
                nc.scalar.copy(out=columns, in_=flipped[:].rearrange("q u n -> q n u"))
            else:
                nc.vector.tensor_copy(out=columns, in_=flipped[:].rearrange("q u n -> q n u"))

        def new_grouped():
            return stage.tile([P, BLOCK * PACK], BF16, name="grouped", align_bytes=64)

        def quantise(values, codes, scales):
            nc.vector.quantize_mx(out=codes[:].bitcast(FP8X4), scales=scales[:], in_=values[:])

        def quantise_half(values, codes, scales, half):
            cols = slice(half * PAIR, (half + 1) * PAIR)
            nc.vector.quantize_mx(
                out=codes[:, cols].bitcast(FP8X4),
                scales=scales[:, cols],
                in_=values[:, half * PAIR * PACK : (half + 1) * PAIR * PACK],
            )

        def quantise_pair(pair):
            quantise_half(x_grouped[pair // 2], x_codes[pair // 2], x_scales[pair // 2], pair % 2)

        def flip_pair(pair, tag="flipped"):
            x_flipped[pair] = flip(x_rows[pair // 2][:], pair % 2, tag)

        def regroup_tile(tile, on_scalar):
            pair, c = divmod(tile, 2)
            if tile % 4 == 0:
                x_grouped[pair // 2] = new_grouped()
            first = (tile % 4) * P
            columns = x_grouped[pair // 2][:].bitcast(F32).rearrange("q (n u) -> q n u", u=2)[:, first : first + P, :]
            words = x_flipped[pair][:].rearrange("q u n -> q n u")[:, c * P : (c + 1) * P, :]
            if on_scalar:
                nc.scalar.copy(out=columns, in_=words)
            else:
                nc.vector.tensor_copy(out=columns, in_=words)

        def regroup_pair(pair, on_scalar=False):
            if pair % 2 == 0:
                x_grouped[pair // 2] = new_grouped()
            regroup(x_flipped[pair], x_grouped[pair // 2], pair % 2, on_scalar)

        def first_matmul(unit, tag="sums"):
            b, j = divmod(unit, TILES)
            sums[unit] = psum.tile([P, BLOCK], F32, name="sums", tag=tag, bufs=PSUM_BUFS[tag])
            nc.tensor.matmul_mx(
                out=sums[unit][:],
                lhsT=w_codes[:, j * P : (j + 1) * P].bitcast(FP8X4),
                lhsT_scale=w_scales[:, j * P : (j + 1) * P],
                rhs=x_codes[b][:].bitcast(FP8X4),
                rhs_scale=x_scales[b][:],
                start=True,
                stop=True,
            )

        def relu(unit):
            b, j = divmod(unit, TILES)
            if j == 0:
                h[b] = hidden.tile([P, TILES, BLOCK], F32, name="h")
            nc.scalar.activation(out=h[b][:, j, :], in_=sums[unit][:], func=ACT.Relu, bias=bias[:, j : j + 1], scale=1.0)

        def transpose_back(t):
            b, c = divmod(t, TILES)
            h_rows[t] = psum.tile([P, TILES, P], F32, name="h_rows", tag="h_rows", bufs=PSUM_BUFS["h_rows"])
            for j in range(TILES):
                nc.tensor.transpose(h_rows[t][:, j, :], h[b][:, j, c * P : (c + 1) * P], ident[:])

        def reciprocal_norm(t):
            squares = stage.tile([P, BLOCK], BF16, name="squares")
            sum_sq = small.tile([P, 1], F32, name="sum_sq")
            nc.scalar.activation(
                out=squares[:], in_=h_rows[t][:].rearrange("p j d -> p (j d)"), func=ACT.Square, accum_out=sum_sq[:]
            )
            floored = small.tile([P, 1], F32, name="floored")
            nc.gpsimd.tensor_scalar_max(out=floored[:], in0=sum_sq[:], scalar1=EPS * EPS)
            inv_norm[t] = small.tile([P, 1], F32, name="inv_norm")
            nc.gpsimd.tensor_tensor(out=inv_norm[t][:], in0=floored[:], in1=minus_half[:], op=ALU.pow)

        def spread_norm(t):
            spread[t] = psum.tile([P, P], F32, name="spread", tag="spread", bufs=PSUM_BUFS["spread"])
            nc.tensor.matmul(
                out=spread[t][:], lhsT=inv_norm[t][:].to_broadcast([P, P]), rhs=ident[:], start=True, stop=True
            )

        def scale_hidden(t):
            b, c = divmod(t, TILES)
            xn[t] = stage.tile([P, P * PACK], BF16, name="xn", align_bytes=64)
            nc.vector.tensor_tensor(
                out=xn[t][:].rearrange("p (g i j) -> p g j i", i=RUN, j=PACK),
                in0=h[b][:, :, c * P : (c + 1) * P].rearrange("p j (g i) -> p g j i", i=RUN),
                in1=spread[t][:].rearrange("p (g i) -> p g i", i=RUN).unsqueeze(2).to_broadcast([P, P // RUN, PACK, RUN]),
                op=ALU.mult,
            )

        def quantise_xn(t):
            xn_codes[t] = operands.tile([P, P], U32, name="xn_codes", align_bytes=64)
            xn_scales[t] = operands.tile([P, P], U8, name="xn_scales", align_bytes=64)
            quantise(xn[t], xn_codes[t], xn_scales[t])

        def second_matmul(t):
            logits[t] = psum.tile([P, BLOCK], F32, name="logits", tag="logits", bufs=PSUM_BUFS["logits"])
            nc.tensor.matmul_mx(
                out=logits[t][:],
                lhsT=xn_codes[t][:].bitcast(FP8X4),
                lhsT_scale=xn_scales[t][:],
                rhs=e_codes[:].bitcast(FP8X4),
                rhs_scale=e_scales[:],
                start=True,
                stop=True,
            )

        def row_maximum(t):
            neg_max[t] = small.tile([P, 1], F32, name="neg_max")
            nc.vector.tensor_reduce(
                out=neg_max[t][:], in_=logits[t][:], axis=mybir.AxisListType.X, op=ALU.max, negate=True
            )

        def exponentials(t):
            probs[t] = results.tile([P, BLOCK], F32, name="probs")
            if t % 2 == 0:
                sums2[t // 2] = small.tile([P, 2], F32, name="exp_sum")
            exp_sum[t] = sums2[t // 2][:, t % 2 : t % 2 + 1]
            nc.scalar.activation(
                out=probs[t][:], in_=logits[t][:], func=ACT.Exp, bias=neg_max[t][:], scale=1.0, accum_out=exp_sum[t]
            )

        def reciprocal_sums(t):
            both = small.tile([P, 2], F32, name="inv_sum")
            nc.vector.reciprocal(out=both[:], in_=sums2[t // 2][:])
            for i in range(2):
                inv_sum[t + i] = both[:, i : i + 1]

        def divide_and_store(t):
            b, c = divmod(t, TILES)
            if on_gpsimd(t):
                nc.gpsimd.tensor_scalar(
                    out=probs[t][:], in0=probs[t][:], scalar1=inv_sum[t], scalar2=0.0, op0=ALU.mult, op1=ALU.add
                )
            elif 24 <= t < 28:
                nc.scalar.activation(out=probs[t][:], in_=probs[t][:], func=ACT.Copy, scale=inv_sum[t])
            else:
                nc.vector.tensor_scalar_mul(out=probs[t][:], in0=probs[t][:], scalar1=inv_sum[t])
            nc.sync.dma_start(out=out_blocks[b][:, c, :], in_=probs[t][:])

        w_grouped[0] = new_grouped()
        e_grouped[0] = new_grouped()
        w_flipped[0] = flip(w_rows[:], 0, "logits")
        keep_busy()
        flip_pair(0, "flipped")
        keep_busy()
        flip_pair(1, "h_rows")
        keep_busy()
        w_flipped[1] = flip(w_rows[:], 1, "logits")
        regroup(w_flipped[0], w_grouped[0], 0, True)
        regroup_pair(0, False)
        regroup_pair(1, True)
        quantise_half(w_grouped[0], w_codes, w_scales, 0)
        quantise_pair(0)
        quantise_pair(1)
        regroup(w_flipped[1], w_grouped[0], 1, True)
        quantise_half(w_grouped[0], w_codes, w_scales, 1)
        flip_pair(2, "logits")
        flip_pair(3, "flipped")
        first_matmul(0)
        relu(0)
        first_matmul(1)
        relu(1)
        first_matmul(2, "logits")
        relu(2)
        first_matmul(3, "logits")
        relu(3)
        regroup_pair(2, False)
        regroup_pair(3, False)
        quantise_pair(2)
        quantise_pair(3)
        flip_pair(4, "logits")
        flip_pair(5, "spread")
        first_matmul(4)
        relu(4)
        first_matmul(5)
        relu(5)
        transpose_back(0)
        regroup_pair(4, False)
        regroup_pair(5, False)
        quantise_pair(4)
        quantise_pair(5)
        e_flipped[0] = flip(e_rows[:], 0, "logits")
        e_flipped[1] = flip(e_rows[:], 1, "flipped")
        first_matmul(6)
        regroup(e_flipped[0], e_grouped[0], 0, False)
        regroup(e_flipped[1], e_grouped[0], 1, False)
        flip_pair(6, "logits")
        quantise(e_grouped[0], e_codes, e_scales)

        for step in range(STEPS):
            tile = step + 12
            if due(step, 7, UNITS) and on_gpsimd(step - 7):
                divide_and_store(step - 7)
            if due(step, 2, UNITS):
                scale_hidden(step - 2)
            if due(step, 0, UNITS):
                reciprocal_norm(step)
            if due(step, 5, UNITS):
                exponentials(step - 5)
            if due(step, -HIDDEN_AHEAD, UNITS):
                relu(step + HIDDEN_AHEAD)
            if due(step, 4, UNITS):
                row_maximum(step - 4)
            if due(step, 3, UNITS):
                second_matmul(step - 3)
            if due(step, -HIDDEN_AHEAD - 1, UNITS):
                first_matmul(step + HIDDEN_AHEAD + 1)
            if due(step, 1, UNITS):
                spread_norm(step - 1)
            if due(step, 7, UNITS) and not on_gpsimd(step - 7):
                divide_and_store(step - 7)
            if tile < UNITS:
                regroup_tile(tile, tile % 2 == 0)
            if due(step, -1, UNITS):
                transpose_back(step + 1)
            if tile % 2 == 1 and tile + 1 < UNITS:
                flip_pair((tile + 1) // 2)
            if tile % 2 == 0 and 14 <= tile < UNITS + 2:
                quantise_pair(tile // 2 - 1)
            if due(step, 2, UNITS):
                quantise_xn(step - 2)
            if due(step, 6, UNITS) and step % 2 == 0:
                reciprocal_sums(step - 6)
